import numpy as np
import ml_dtypes


def mxq(x, axis, fmt="e4m3"):
    dtype, down = {"e4m3": (ml_dtypes.float8_e4m3fn, 7), "e5m2": (ml_dtypes.float8_e5m2, 14)}[fmt]
    v = np.moveaxis(np.asarray(x, np.float32).astype(ml_dtypes.bfloat16).astype(np.float64), axis, -1)
    blocks = v.reshape(v.shape[:-1] + (-1, 32))
    amax = np.abs(blocks).max(-1, keepdims=True)
    byte = np.maximum(np.where(amax > 0, np.frexp(amax)[1] - 1 + 127, 0) - down, 1)
    scale = np.exp2(byte - 127.0)
    codes = (blocks / scale).astype(np.float32).astype(dtype).astype(np.float64)
    return np.moveaxis((codes * scale).reshape(v.shape), -1, axis)


BF16 = ml_dtypes.bfloat16


def bf(x):
    return np.asarray(x, np.float32).astype(BF16)


def f64(x):
    return np.asarray(x).astype(np.float64)


B, D, HH, WW = 4, 256, 128, 128
M = HH * WW


def setup_inputs():
    n = np.random.standard_normal((B, D, HH, WW))
    g = np.random.standard_normal((B, HH, WW))[:, None]
    a = np.random.standard_normal((B, D))[:, :, None, None]
    mu = np.random.standard_normal((B, D))[:, :, None, None]
    return {"x": bf(n + a * g + mu)}


def reference(x):
    xf = f64(x).reshape(B, D, M)
    inv_m = 1.0 / M
    xi = inv_m * xf - (inv_m * inv_m) * xf.sum(-1, keepdims=True)
    return mxq(xi, 2, "e4m3") @ mxq(xf, 2, "e4m3").transpose(0, 2, 1)

@@ -1,0 +1,241 @@
+from contextlib import ExitStack
+
+import concourse.mybir as mybir
+from concourse.masks import make_identity
+
+FLOPS = 2 * 4 * 256 * 256 * 16384
+
+BF16 = mybir.dt.bfloat16
+F32 = mybir.dt.float32
+U32 = mybir.dt.uint32
+U8 = mybir.dt.uint8
+FP8X4 = mybir.dt.float8_e4m3fn_x4
+ADD = mybir.AluOpType.add
+MULT = mybir.AluOpType.mult
+
+P = 128
+PACK = 4
+K_PASS = P * PACK
+IMAGES = 4
+CH = 256
+HALVES = CH // P
+POS = 128 * 128
+PASSES = POS // K_PASS
+RUN = 4
+ROUND_K = RUN * K_PASS
+ROUNDS = PASSES // RUN
+ALL_ROUNDS = IMAGES * ROUNDS
+ALL_PASSES = IMAGES * PASSES
+GROUPS = PACK * CH // P
+GROUP_CH = CH // GROUPS
+
+SUM_LAG = 2
+XI_LAG = ROUNDS + 1
+MX_LAG = 1
+PREFETCH = 4
+
+X_BUFS = XI_LAG + PREFETCH
+XF_KEPT = RUN * (XI_LAG + MX_LAG + 1)
+
+
+def tile_covpool_pa_k_kernel(tc, x, out):
+    nc = tc.nc
+    positions = x.rearrange("b c i j -> b c (i j)")
+
+    with ExitStack() as ctx:
+        consts = ctx.enter_context(tc.tile_pool(name="consts", bufs=1))
+        x_pool = ctx.enter_context(tc.tile_pool(name="x", bufs=X_BUFS))
+        xi_pool = ctx.enter_context(tc.tile_pool(name="xi", bufs=2))
+        xf_grouped_pool = ctx.enter_context(tc.tile_pool(name="xf_grouped", bufs=RUN + SUM_LAG))
+        xi_grouped_pool = ctx.enter_context(tc.tile_pool(name="xi_grouped", bufs=RUN))
+        xf_kept_pool = ctx.enter_context(tc.tile_pool(name="xf_kept", bufs=XF_KEPT))
+        xi_quantised_pool = ctx.enter_context(tc.tile_pool(name="xi_quantised", bufs=2 * RUN))
+        mean_pool = ctx.enter_context(tc.tile_pool(name="mean", bufs=2))
+        y_pool = ctx.enter_context(tc.tile_pool(name="y", bufs=2))
+        ring = ctx.enter_context(tc.psum_pool(name="ring", bufs=5))
+        sums_psum = ctx.enter_context(tc.psum_pool(name="sums", bufs=1))
+        y_psum = ctx.enter_context(tc.psum_pool(name="products", bufs=1))
+        ctx.enter_context(tc.manual_schedule())
+
+        ident = consts.tile([P, P], F32)
+        make_identity(nc, ident[:])
+        pick = consts.tile([P, GROUPS, GROUPS], BF16)
+        nc.vector.memset(pick[:], 0.0)
+        for q in range(GROUPS):
+            nc.vector.memset(pick[:, q, q : q + 1], 1.0)
+        same_channel = consts.tile([P, GROUP_CH], F32)
+        nc.vector.tensor_reduce(
+            out=same_channel[:],
+            in_=ident[:].rearrange("p (c t) -> p c t", t=PACK),
+            axis=mybir.AxisListType.X,
+            op=ADD,
+        )
+        minus_inv_pos = consts.tile([P, 1], F32)
+        nc.vector.memset(minus_inv_pos[:], -1.0 / POS)
+
+        x_tiles = {}
+        xi_tiles = {}
+        xf_grouped = {}
+        xi_grouped = {}
+        xf_kept = {}
+        xi_quantised = {}
+        sums_banks = {}
+        spreads = {}
+        mean_banks = {}
+        neg_means = {}
+        y_banks = {}
+
+        def load_round(rnd):
+            b, r = divmod(rnd, ROUNDS)
+            x_tile = x_pool.tile([P, HALVES, ROUND_K], BF16)
+            nc.sync.dma_start(
+                out=x_tile[:],
+                in_=positions[b, :, r * ROUND_K : (r + 1) * ROUND_K].rearrange("(h p) k -> p h k", p=P),
+            )
+            x_tiles[rnd] = x_tile
+
+        def transpose_pass(source, i, grouped):
+            words = source[:].bitcast(F32)
+            bank = ring.tile([P, 2, CH], F32, tag="bank")
+            for h in range(HALVES):
+                for u in range(2):
+                    first = (K_PASS // 2) * i + P * u
+                    nc.tensor.transpose(
+                        bank[:, u, P * h : P * (h + 1)], words[:, h, first : first + P], ident[:]
+                    )
+            nc.scalar.copy(
+                out=grouped[:].bitcast(F32).rearrange("p (c u) -> p c u", u=2),
+                in_=bank[:].rearrange("p u c -> p c u"),
+            )
+
+        def quantise(grouped, pool):
+            codes = pool.tile([P, CH], U32, align_bytes=64)
+            scales = pool.tile([P, CH], U8, align_bytes=64)
+            nc.vector.quantize_mx(out=codes[:].bitcast(FP8X4), scales=scales[:], in_=grouped[:])
+            return codes, scales
+
+        def add_to_sums(m):
+            b, g = divmod(m, PASSES)
+            if g == 0:
+                sums_bank = sums_psum.tile([P, GROUPS], F32)
+                sums_banks[b] = sums_bank
+            for q in range(GROUPS):
+                nc.tensor.matmul(
+                    sums_banks[b][:],
+                    lhsT=xf_grouped[m][:, P * q : P * (q + 1)],
+                    rhs=pick[:, q, :],
+                    start=(g == 0 and q == 0),
+                    stop=(g == PASSES - 1 and q == GROUPS - 1),
+                )
+
+        def spread_sums(b):
+            spread = mean_pool.tile([P, CH], F32)
+            nc.vector.tensor_tensor(
+                out=spread[:].rearrange("p (q c) -> p q c", q=GROUPS),
+                in0=same_channel[:].unsqueeze(1).to_broadcast([P, GROUPS, GROUP_CH]),
+                in1=sums_banks[b][:].unsqueeze(2).to_broadcast([P, GROUPS, GROUP_CH]),
+                op=MULT,
+            )
+            spreads[b] = spread
+
+        def gather_means(b):
+            mean_bank = ring.tile([P, HALVES], F32, tag="bank")
+            for h in range(HALVES):
+                nc.tensor.matmul(
+                    mean_bank[:, h : h + 1],
+                    lhsT=spreads[b][:, P * h : P * (h + 1)],
+                    rhs=minus_inv_pos[:],
+                    start=True,
+                    stop=True,
+                )
+            mean_banks[b] = mean_bank
+
+        def form_xi(rnd):
+            b = rnd // ROUNDS
+            xi_tile = xi_pool.tile([P, HALVES, ROUND_K], BF16)
+            for h in range(HALVES):
+                nc.vector.tensor_scalar(
+                    out=xi_tile[:, h, :],
+                    in0=x_tiles[rnd][:, h, :],
+                    scalar1=neg_means[b][:, h : h + 1],
+                    scalar2=1.0 / POS,
+                    op0=ADD,
+                    op1=MULT,
+                )
+            xi_tiles[rnd] = xi_tile
+
+        def multiply_pass(m):
+            b, g = divmod(m, PASSES)
+            xi_codes, xi_scales = xi_quantised[m]
+            xf_codes, xf_scales = xf_kept[m]
+            for h in range(HALVES):
+                if g == 0:
+                    y_bank = y_psum.tile([P, CH], F32, tag="y%d" % h)
+                    y_banks[b, h] = y_bank
+                nc.tensor.matmul_mx(
+                    out=y_banks[b, h][:],
+                    lhsT=xi_codes[:, P * h : P * (h + 1)].bitcast(FP8X4),
+                    lhsT_scale=xi_scales[:, P * h : P * (h + 1)],
+                    rhs=xf_codes[:].bitcast(FP8X4),
+                    rhs_scale=xf_scales[:],
+                    start=(g == 0),
+                    stop=(g == PASSES - 1),
+                )
+
+        def store_image(b):
+            y_sb = y_pool.tile([P, HALVES, CH], F32)
+            for h in range(HALVES):
+                nc.vector.tensor_copy(out=y_sb[:, h, :], in_=y_banks[b, h][:])
+            nc.sync.dma_start(out=out[b].rearrange("(h p) n -> p h n", p=P), in_=y_sb[:])
+
+        for rnd in range(PREFETCH):
+            load_round(rnd)
+
+        for step in range(ALL_ROUNDS + XI_LAG + MX_LAG):
+            first_trip = step
+            second_trip = step - XI_LAG
+            multiplied = second_trip - MX_LAG
+            summed_image = step // ROUNDS - 1 if step % ROUNDS == 0 else -1
+
+            if step + PREFETCH < ALL_ROUNDS:
+                load_round(step + PREFETCH)
+
+            for i in range(RUN):
+                m = RUN * first_trip + i
+                if m < ALL_PASSES:
+                    grouped = xf_grouped_pool.tile([P, PACK * CH], BF16, align_bytes=64)
+                    transpose_pass(x_tiles[first_trip], i, grouped)
+                    xf_grouped[m] = grouped
+                if 0 <= m - SUM_LAG < ALL_PASSES:
+                    add_to_sums(m - SUM_LAG)
+                    if (m - SUM_LAG) % PASSES == PASSES - 1:
+                        spread_sums((m - SUM_LAG) // PASSES)
+
+            if 0 <= second_trip < ALL_ROUNDS:
+                for i in range(RUN):
+                    grouped = xi_grouped_pool.tile([P, PACK * CH], BF16, align_bytes=64)
+                    transpose_pass(xi_tiles[second_trip], i, grouped)
+                    xi_grouped[RUN * second_trip + i] = grouped
+
+            if 0 <= summed_image < IMAGES:
+                gather_means(summed_image)
+            if 0 <= multiplied < ALL_ROUNDS:
+                for i in range(RUN):
+                    multiply_pass(RUN * multiplied + i)
+
+            if first_trip < ALL_ROUNDS:
+                for i in range(RUN):
+                    m = RUN * first_trip + i
+                    xf_kept[m] = quantise(xf_grouped[m], xf_kept_pool)
+            if 0 <= summed_image < IMAGES:
+                neg_mean = mean_pool.tile([P, HALVES], F32)
+                nc.vector.tensor_copy(out=neg_mean[:], in_=mean_banks[summed_image][:])
+                neg_means[summed_image] = neg_mean
+            if 0 <= second_trip + 1 < ALL_ROUNDS:
+                form_xi(second_trip + 1)
+            if 0 <= second_trip < ALL_ROUNDS:
+                for i in range(RUN):
+                    m = RUN * second_trip + i
+                    xi_quantised[m] = quantise(xi_grouped[m], xi_quantised_pool)
+            if 0 <= multiplied < ALL_ROUNDS and multiplied % ROUNDS == ROUNDS - 1:
+                store_image(multiplied // ROUNDS)

@@ -28,6 +28,7 @@ ALL_ROUNDS = IMAGES * ROUNDS
 ALL_PASSES = IMAGES * PASSES
 GROUPS = PACK * CH // P
 GROUP_CH = CH // GROUPS
+SUM_COLS = 20
 
 SUM_LAG = 2
 XI_LAG = ROUNDS + 1
@@ -59,7 +60,7 @@ def tile_covpool_pa_k_kernel(tc, x, out):
 
         ident = consts.tile([P, P], F32)
         make_identity(nc, ident[:])
-        pick = consts.tile([P, GROUPS, GROUPS], BF16)
+        pick = consts.tile([P, GROUPS, SUM_COLS], BF16)
         nc.vector.memset(pick[:], 0.0)
         for q in range(GROUPS):
             nc.vector.memset(pick[:, q, q : q + 1], 1.0)
@@ -117,7 +118,7 @@ def tile_covpool_pa_k_kernel(tc, x, out):
         def add_to_sums(m):
             b, g = divmod(m, PASSES)
             if g == 0:
-                sums_bank = sums_psum.tile([P, GROUPS], F32)
+                sums_bank = sums_psum.tile([P, SUM_COLS], F32)
                 sums_banks[b] = sums_bank
             for q in range(GROUPS):
                 nc.tensor.matmul(
@@ -133,7 +134,7 @@ def tile_covpool_pa_k_kernel(tc, x, out):
             nc.vector.tensor_tensor(
                 out=spread[:].rearrange("p (q c) -> p q c", q=GROUPS),
                 in0=same_channel[:].unsqueeze(1).to_broadcast([P, GROUPS, GROUP_CH]),
-                in1=sums_banks[b][:].unsqueeze(2).to_broadcast([P, GROUPS, GROUP_CH]),
+                in1=sums_banks[b][:, 0:GROUPS].unsqueeze(2).to_broadcast([P, GROUPS, GROUP_CH]),
                 op=MULT,
             )
             spreads[b] = spread

@@ -28,12 +28,14 @@ ALL_ROUNDS = IMAGES * ROUNDS
 ALL_PASSES = IMAGES * PASSES
 GROUPS = PACK * CH // P
 GROUP_CH = CH // GROUPS
-SUM_COLS = 20
+SUM_COLS = 24
 
-SUM_LAG = 2
+SUM_LAG = 1
 XI_LAG = ROUNDS + 1
 MX_LAG = 1
 PREFETCH = 4
+WARM_PASSES = 14
+WARM_COLS = 512
 
 X_BUFS = XI_LAG + PREFETCH
 XF_KEPT = RUN * (XI_LAG + MX_LAG + 1)
@@ -47,7 +49,7 @@ def tile_covpool_pa_k_kernel(tc, x, out):
         consts = ctx.enter_context(tc.tile_pool(name="consts", bufs=1))
         x_pool = ctx.enter_context(tc.tile_pool(name="x", bufs=X_BUFS))
         xi_pool = ctx.enter_context(tc.tile_pool(name="xi", bufs=2))
-        xf_grouped_pool = ctx.enter_context(tc.tile_pool(name="xf_grouped", bufs=RUN + SUM_LAG))
+        xf_grouped_pool = ctx.enter_context(tc.tile_pool(name="xf_grouped", bufs=RUN * (1 + SUM_LAG)))
         xi_grouped_pool = ctx.enter_context(tc.tile_pool(name="xi_grouped", bufs=RUN))
         xf_kept_pool = ctx.enter_context(tc.tile_pool(name="xf_kept", bufs=XF_KEPT))
         xi_quantised_pool = ctx.enter_context(tc.tile_pool(name="xi_quantised", bufs=2 * RUN))
@@ -57,6 +59,23 @@ def tile_covpool_pa_k_kernel(tc, x, out):
         sums_psum = ctx.enter_context(tc.psum_pool(name="sums", bufs=1))
         y_psum = ctx.enter_context(tc.psum_pool(name="products", bufs=1))
         ctx.enter_context(tc.manual_schedule())
+
+        warm_codes = consts.tile([P, WARM_COLS], U32, align_bytes=64)
+        warm_scales = consts.tile([P, WARM_COLS], U8, align_bytes=64)
+        warm_zeros = consts.tile([P, PACK * WARM_COLS], BF16, align_bytes=64)
+        nc.vector.memset(warm_zeros[:], 0.0)
+        nc.vector.quantize_mx(out=warm_codes[:].bitcast(FP8X4), scales=warm_scales[:], in_=warm_zeros[:])
+        warm_bank = ring.tile([P, WARM_COLS], F32, tag="bank")
+        for w in range(WARM_PASSES):
+            nc.tensor.matmul_mx(
+                out=warm_bank[:],
+                lhsT=warm_codes[:, 0:P].bitcast(FP8X4),
+                lhsT_scale=warm_scales[:, 0:P],
+                rhs=warm_codes[:].bitcast(FP8X4),
+                rhs_scale=warm_scales[:],
+                start=True,
+                stop=True,
+            )
 
         ident = consts.tile([P, P], F32)
         make_identity(nc, ident[:])
@@ -194,41 +213,41 @@ def tile_covpool_pa_k_kernel(tc, x, out):
 
         for step in range(ALL_ROUNDS + XI_LAG + MX_LAG):
             first_trip = step
+            summed = first_trip - SUM_LAG
             second_trip = step - XI_LAG
             multiplied = second_trip - MX_LAG
-            summed_image = step // ROUNDS - 1 if step % ROUNDS == 0 else -1
+            summed_image = summed // ROUNDS if summed % ROUNDS == ROUNDS - 1 and summed < ALL_ROUNDS else -1
 
             if step + PREFETCH < ALL_ROUNDS:
                 load_round(step + PREFETCH)
 
-            for i in range(RUN):
-                m = RUN * first_trip + i
-                if m < ALL_PASSES:
+            if first_trip < ALL_ROUNDS:
+                for i in range(RUN):
                     grouped = xf_grouped_pool.tile([P, PACK * CH], BF16, align_bytes=64)
                     transpose_pass(x_tiles[first_trip], i, grouped)
-                    xf_grouped[m] = grouped
-                if 0 <= m - SUM_LAG < ALL_PASSES:
-                    add_to_sums(m - SUM_LAG)
-                    if (m - SUM_LAG) % PASSES == PASSES - 1:
-                        spread_sums((m - SUM_LAG) // PASSES)
+                    xf_grouped[RUN * first_trip + i] = grouped
+            if 0 <= summed < ALL_ROUNDS:
+                for i in range(RUN):
+                    add_to_sums(RUN * summed + i)
+            if first_trip < ALL_ROUNDS:
+                for i in range(RUN):
+                    m = RUN * first_trip + i
+                    xf_kept[m] = quantise(xf_grouped[m], xf_kept_pool)
+            if summed_image >= 0:
+                spread_sums(summed_image)
 
             if 0 <= second_trip < ALL_ROUNDS:
                 for i in range(RUN):
                     grouped = xi_grouped_pool.tile([P, PACK * CH], BF16, align_bytes=64)
                     transpose_pass(xi_tiles[second_trip], i, grouped)
                     xi_grouped[RUN * second_trip + i] = grouped
-
-            if 0 <= summed_image < IMAGES:
+            if summed_image >= 0:
                 gather_means(summed_image)
             if 0 <= multiplied < ALL_ROUNDS:
                 for i in range(RUN):
                     multiply_pass(RUN * multiplied + i)
 
-            if first_trip < ALL_ROUNDS:
-                for i in range(RUN):
-                    m = RUN * first_trip + i
-                    xf_kept[m] = quantise(xf_grouped[m], xf_kept_pool)
-            if 0 <= summed_image < IMAGES:
+            if summed_image >= 0:
                 neg_mean = mean_pool.tile([P, HALVES], F32)
                 nc.vector.tensor_copy(out=neg_mean[:], in_=mean_banks[summed_image][:])
                 neg_means[summed_image] = neg_mean

@@ -9,6 +9,7 @@ BF16 = mybir.dt.bfloat16
 F32 = mybir.dt.float32
 U32 = mybir.dt.uint32
 U8 = mybir.dt.uint8
+I32 = mybir.dt.int32
 FP8X4 = mybir.dt.float8_e4m3fn_x4
 ADD = mybir.AluOpType.add
 MULT = mybir.AluOpType.mult
@@ -34,8 +35,8 @@ SUM_LAG = 1
 XI_LAG = ROUNDS + 1
 MX_LAG = 1
 PREFETCH = 4
-WARM_PASSES = 14
-WARM_COLS = 512
+WARM_PASSES = 28
+FILL_PASSES = 4
 
 X_BUFS = XI_LAG + PREFETCH
 XF_KEPT = RUN * (XI_LAG + MX_LAG + 1)
@@ -60,22 +61,26 @@ def tile_covpool_pa_k_kernel(tc, x, out):
         y_psum = ctx.enter_context(tc.psum_pool(name="products", bufs=1))
         ctx.enter_context(tc.manual_schedule())
 
-        warm_codes = consts.tile([P, WARM_COLS], U32, align_bytes=64)
-        warm_scales = consts.tile([P, WARM_COLS], U8, align_bytes=64)
-        warm_zeros = consts.tile([P, PACK * WARM_COLS], BF16, align_bytes=64)
-        nc.vector.memset(warm_zeros[:], 0.0)
-        nc.vector.quantize_mx(out=warm_codes[:].bitcast(FP8X4), scales=warm_scales[:], in_=warm_zeros[:])
-        warm_bank = ring.tile([P, WARM_COLS], F32, tag="bank")
-        for w in range(WARM_PASSES):
-            nc.tensor.matmul_mx(
-                out=warm_bank[:],
-                lhsT=warm_codes[:, 0:P].bitcast(FP8X4),
-                lhsT_scale=warm_scales[:, 0:P],
-                rhs=warm_codes[:].bitcast(FP8X4),
-                rhs_scale=warm_scales[:],
-                start=True,
-                stop=True,
-            )
+        zeros = consts.tile([P, PACK * CH], BF16, align_bytes=64)
+        zero_codes = consts.tile([P, CH], U32, align_bytes=64)
+        zero_scales = consts.tile([P, CH], U8, align_bytes=64)
+        nc.vector.memset(zeros[:].bitcast(I32), 0)
+        nc.vector.quantize_mx(out=zero_codes[:].bitcast(FP8X4), scales=zero_scales[:], in_=zeros[:])
+
+        def idle_passes(count):
+            idle_bank = ring.tile([P, CH], F32, tag="bank")
+            for w in range(count):
+                nc.tensor.matmul_mx(
+                    out=idle_bank[:],
+                    lhsT=zero_codes[:, 0:P].bitcast(FP8X4),
+                    lhsT_scale=zero_scales[:, 0:P],
+                    rhs=zero_codes[:].bitcast(FP8X4),
+                    rhs_scale=zero_scales[:],
+                    start=True,
+                    stop=True,
+                )
+
+        idle_passes(WARM_PASSES)
 
         ident = consts.tile([P, P], F32)
         make_identity(nc, ident[:])
@@ -114,7 +119,7 @@ def tile_covpool_pa_k_kernel(tc, x, out):
             )
             x_tiles[rnd] = x_tile
 
-        def transpose_pass(source, i, grouped):
+        def transpose_pass(source, i, grouped, empty_bank):
             words = source[:].bitcast(F32)
             bank = ring.tile([P, 2, CH], F32, tag="bank")
             for h in range(HALVES):
@@ -123,7 +128,7 @@ def tile_covpool_pa_k_kernel(tc, x, out):
                     nc.tensor.transpose(
                         bank[:, u, P * h : P * (h + 1)], words[:, h, first : first + P], ident[:]
                     )
-            nc.scalar.copy(
+            empty_bank(
                 out=grouped[:].bitcast(F32).rearrange("p (c u) -> p c u", u=2),
                 in_=bank[:].rearrange("p u c -> p c u"),
             )
@@ -224,11 +229,15 @@ def tile_covpool_pa_k_kernel(tc, x, out):
             if first_trip < ALL_ROUNDS:
                 for i in range(RUN):
                     grouped = xf_grouped_pool.tile([P, PACK * CH], BF16, align_bytes=64)
-                    transpose_pass(x_tiles[first_trip], i, grouped)
+                    transpose_pass(
+                        x_tiles[first_trip], i, grouped, nc.vector.tensor_copy if i == RUN - 1 else nc.scalar.copy
+                    )
                     xf_grouped[RUN * first_trip + i] = grouped
             if 0 <= summed < ALL_ROUNDS:
                 for i in range(RUN):
                     add_to_sums(RUN * summed + i)
+            elif first_trip < ALL_ROUNDS:
+                idle_passes(FILL_PASSES)
             if first_trip < ALL_ROUNDS:
                 for i in range(RUN):
                     m = RUN * first_trip + i
@@ -239,13 +248,15 @@ def tile_covpool_pa_k_kernel(tc, x, out):
             if 0 <= second_trip < ALL_ROUNDS:
                 for i in range(RUN):
                     grouped = xi_grouped_pool.tile([P, PACK * CH], BF16, align_bytes=64)
-                    transpose_pass(xi_tiles[second_trip], i, grouped)
+                    transpose_pass(xi_tiles[second_trip], i, grouped, nc.scalar.copy)
                     xi_grouped[RUN * second_trip + i] = grouped
             if summed_image >= 0:
                 gather_means(summed_image)
             if 0 <= multiplied < ALL_ROUNDS:
                 for i in range(RUN):
                     multiply_pass(RUN * multiplied + i)
+            elif 0 <= second_trip < ALL_ROUNDS:
+                idle_passes(FILL_PASSES)
 
             if summed_image >= 0:
                 neg_mean = mean_pool.tile([P, HALVES], F32)

@@ -22,6 +22,7 @@ CH = 256
 HALVES = CH // P
 POS = 128 * 128
 PASSES = POS // K_PASS
+PAIR = 2
 RUN = 4
 ROUND_K = RUN * K_PASS
 ROUNDS = PASSES // RUN
@@ -34,12 +35,13 @@ SUM_COLS = 24
 SUM_LAG = 1
 XI_LAG = ROUNDS + 1
 MX_LAG = 1
-PREFETCH = 4
+PREFETCH = 3
+SHORT_ROUNDS = ALL_ROUNDS - XI_LAG
 WARM_PASSES = 28
 FILL_PASSES = 4
 
-X_BUFS = XI_LAG + PREFETCH
-XF_KEPT = RUN * (XI_LAG + MX_LAG + 1)
+X_BUFS = XI_LAG - 1 + PREFETCH
+XF_KEPT = XI_LAG + MX_LAG + 1
 
 
 def tile_covpool_pa_k_kernel(tc, x, out):
@@ -50,10 +52,13 @@ def tile_covpool_pa_k_kernel(tc, x, out):
         consts = ctx.enter_context(tc.tile_pool(name="consts", bufs=1))
         x_pool = ctx.enter_context(tc.tile_pool(name="x", bufs=X_BUFS))
         xi_pool = ctx.enter_context(tc.tile_pool(name="xi", bufs=2))
-        xf_grouped_pool = ctx.enter_context(tc.tile_pool(name="xf_grouped", bufs=RUN * (1 + SUM_LAG)))
-        xi_grouped_pool = ctx.enter_context(tc.tile_pool(name="xi_grouped", bufs=RUN))
-        xf_kept_pool = ctx.enter_context(tc.tile_pool(name="xf_kept", bufs=XF_KEPT))
-        xi_quantised_pool = ctx.enter_context(tc.tile_pool(name="xi_quantised", bufs=2 * RUN))
+        xf_pair_pool = ctx.enter_context(tc.tile_pool(name="xf_pair", bufs=1 + SUM_LAG))
+        xf_single_pool = ctx.enter_context(tc.tile_pool(name="xf_single", bufs=1 + SUM_LAG))
+        xf_last_pool = ctx.enter_context(tc.tile_pool(name="xf_last", bufs=XI_LAG + 1))
+        xi_pair_pool = ctx.enter_context(tc.tile_pool(name="xi_pair", bufs=3))
+        xf_kept_pair_pool = ctx.enter_context(tc.tile_pool(name="xf_kept_pair", bufs=XF_KEPT))
+        xf_kept_single_pool = ctx.enter_context(tc.tile_pool(name="xf_kept_single", bufs=2 * XF_KEPT))
+        xi_quantised_pool = ctx.enter_context(tc.tile_pool(name="xi_quantised", bufs=2 * RUN // PAIR))
         mean_pool = ctx.enter_context(tc.tile_pool(name="mean", bufs=2))
         y_pool = ctx.enter_context(tc.tile_pool(name="y", bufs=2))
         ring = ctx.enter_context(tc.psum_pool(name="ring", bufs=5))
@@ -97,11 +102,15 @@ def tile_covpool_pa_k_kernel(tc, x, out):
         )
         minus_inv_pos = consts.tile([P, 1], F32)
         nc.vector.memset(minus_inv_pos[:], -1.0 / POS)
+        spread_scale = consts.tile([P, P], F32)
+        nc.vector.memset(spread_scale[:], -1.0 / (POS * POS))
 
         x_tiles = {}
         xi_tiles = {}
         xf_grouped = {}
-        xi_grouped = {}
+        xf_tiles = {}
+        xi_pairs = {}
+        mean_rows = {}
         xf_kept = {}
         xi_quantised = {}
         sums_banks = {}
@@ -129,15 +138,15 @@ def tile_covpool_pa_k_kernel(tc, x, out):
                         bank[:, u, P * h : P * (h + 1)], words[:, h, first : first + P], ident[:]
                     )
             empty_bank(
-                out=grouped[:].bitcast(F32).rearrange("p (c u) -> p c u", u=2),
+                out=grouped.bitcast(F32).rearrange("p (c u) -> p c u", u=2),
                 in_=bank[:].rearrange("p u c -> p c u"),
             )
 
-        def quantise(grouped, pool):
-            codes = pool.tile([P, CH], U32, align_bytes=64)
-            scales = pool.tile([P, CH], U8, align_bytes=64)
+        def quantise(grouped, pool, count):
+            codes = pool.tile([P, count * CH], U32, align_bytes=64)
+            scales = pool.tile([P, count * CH], U8, align_bytes=64)
             nc.vector.quantize_mx(out=codes[:].bitcast(FP8X4), scales=scales[:], in_=grouped[:])
-            return codes, scales
+            return [(codes[:, CH * j : CH * (j + 1)], scales[:, CH * j : CH * (j + 1)]) for j in range(count)]
 
         def add_to_sums(m):
             b, g = divmod(m, PASSES)
@@ -174,20 +183,38 @@ def tile_covpool_pa_k_kernel(tc, x, out):
                     stop=True,
                 )
             mean_banks[b] = mean_bank
+            row_bank = ring.tile([P, CH], F32, tag="bank")
+            nc.tensor.matmul(row_bank[:], lhsT=spread_scale[:], rhs=spreads[b][:], start=True, stop=True)
+            mean_row = mean_pool.tile([P, CH], F32)
+            nc.scalar.copy(out=mean_row[:], in_=row_bank[:])
+            mean_rows[b] = mean_row
 
         def form_xi(rnd):
             b = rnd // ROUNDS
             xi_tile = xi_pool.tile([P, HALVES, ROUND_K], BF16)
+            width = (RUN - 1 if rnd < SHORT_ROUNDS else RUN) * K_PASS
             for h in range(HALVES):
                 nc.vector.tensor_scalar(
-                    out=xi_tile[:, h, :],
-                    in0=x_tiles[rnd][:, h, :],
+                    out=xi_tile[:, h, 0:width],
+                    in0=x_tiles[rnd][:, h, 0:width],
                     scalar1=neg_means[b][:, h : h + 1],
                     scalar2=1.0 / POS,
                     op0=ADD,
                     op1=MULT,
                 )
             xi_tiles[rnd] = xi_tile
+
+        def form_transposed_xi(rnd):
+            pair = xi_pair_pool.tile([P, PAIR * PACK * CH], BF16, align_bytes=64)
+            nc.vector.scalar_tensor_tensor(
+                out=pair[:, PACK * CH :].rearrange("p (c t) -> p c t", t=PACK),
+                in0=xf_tiles[RUN * rnd + RUN - 1][:].rearrange("p (c t) -> p c t", t=PACK),
+                scalar=1.0 / POS,
+                in1=mean_rows[rnd // ROUNDS][:].unsqueeze(2).to_broadcast([P, CH, PACK]),
+                op0=MULT,
+                op1=ADD,
+            )
+            xi_pairs[RUN * rnd + RUN - PAIR] = pair
 
         def multiply_pass(m):
             b, g = divmod(m, PASSES)
@@ -201,8 +228,8 @@ def tile_covpool_pa_k_kernel(tc, x, out):
                     out=y_banks[b, h][:],
                     lhsT=xi_codes[:, P * h : P * (h + 1)].bitcast(FP8X4),
                     lhsT_scale=xi_scales[:, P * h : P * (h + 1)],
-                    rhs=xf_codes[:].bitcast(FP8X4),
-                    rhs_scale=xf_scales[:],
+                    rhs=xf_codes.bitcast(FP8X4),
+                    rhs_scale=xf_scales,
                     start=(g == 0),
                     stop=(g == PASSES - 1),
                 )
@@ -223,33 +250,48 @@ def tile_covpool_pa_k_kernel(tc, x, out):
             multiplied = second_trip - MX_LAG
             summed_image = summed // ROUNDS if summed % ROUNDS == ROUNDS - 1 and summed < ALL_ROUNDS else -1
 
-            if step + PREFETCH < ALL_ROUNDS:
-                load_round(step + PREFETCH)
+            short = 0 <= second_trip < SHORT_ROUNDS
+            if short:
+                form_transposed_xi(second_trip)
 
             if first_trip < ALL_ROUNDS:
                 for i in range(RUN):
-                    grouped = xf_grouped_pool.tile([P, PACK * CH], BF16, align_bytes=64)
+                    m = RUN * first_trip + i
+                    if i == 0:
+                        pair = xf_pair_pool.tile([P, PAIR * PACK * CH], BF16, align_bytes=64)
+                        xf_tiles[m] = pair
+                    elif i == PAIR:
+                        single = xf_single_pool.tile([P, PACK * CH], BF16, align_bytes=64)
+                        xf_tiles[m] = single
+                    elif i == RUN - 1:
+                        last = xf_last_pool.tile([P, PACK * CH], BF16, align_bytes=64)
+                        xf_tiles[m] = last
+                    xf_grouped[m] = pair[:, PACK * CH * i : PACK * CH * (i + 1)] if i < PAIR else xf_tiles[m][:]
+                    by_vector = i == RUN - 1 and not short
                     transpose_pass(
-                        x_tiles[first_trip], i, grouped, nc.vector.tensor_copy if i == RUN - 1 else nc.scalar.copy
+                        x_tiles[first_trip], i, xf_grouped[m], nc.vector.tensor_copy if by_vector else nc.scalar.copy
                     )
-                    xf_grouped[RUN * first_trip + i] = grouped
             if 0 <= summed < ALL_ROUNDS:
                 for i in range(RUN):
                     add_to_sums(RUN * summed + i)
             elif first_trip < ALL_ROUNDS:
                 idle_passes(FILL_PASSES)
             if first_trip < ALL_ROUNDS:
-                for i in range(RUN):
-                    m = RUN * first_trip + i
-                    xf_kept[m] = quantise(xf_grouped[m], xf_kept_pool)
+                m = RUN * first_trip
+                xf_kept[m], xf_kept[m + 1] = quantise(xf_tiles[m], xf_kept_pair_pool, PAIR)
+                for i in range(PAIR, RUN):
+                    xf_kept[m + i] = quantise(xf_tiles[m + i], xf_kept_single_pool, 1)[0]
             if summed_image >= 0:
                 spread_sums(summed_image)
 
             if 0 <= second_trip < ALL_ROUNDS:
-                for i in range(RUN):
-                    grouped = xi_grouped_pool.tile([P, PACK * CH], BF16, align_bytes=64)
+                for i in range(RUN - 1 if short else RUN):
+                    m = RUN * second_trip + i
+                    if i == 0 or i == PAIR and not short:
+                        pair = xi_pair_pool.tile([P, PAIR * PACK * CH], BF16, align_bytes=64)
+                        xi_pairs[m] = pair
+                    grouped = xi_pairs[m - i % PAIR][:, PACK * CH * (i % PAIR) : PACK * CH * (i % PAIR + 1)]
                     transpose_pass(xi_tiles[second_trip], i, grouped, nc.scalar.copy)
-                    xi_grouped[RUN * second_trip + i] = grouped
             if summed_image >= 0:
                 gather_means(summed_image)
             if 0 <= multiplied < ALL_ROUNDS:
@@ -265,8 +307,10 @@ def tile_covpool_pa_k_kernel(tc, x, out):
             if 0 <= second_trip + 1 < ALL_ROUNDS:
                 form_xi(second_trip + 1)
             if 0 <= second_trip < ALL_ROUNDS:
-                for i in range(RUN):
+                for i in range(0, RUN, PAIR):
                     m = RUN * second_trip + i
-                    xi_quantised[m] = quantise(xi_grouped[m], xi_quantised_pool)
+                    xi_quantised[m], xi_quantised[m + 1] = quantise(xi_pairs[m], xi_quantised_pool, PAIR)
             if 0 <= multiplied < ALL_ROUNDS and multiplied % ROUNDS == ROUNDS - 1:
                 store_image(multiplied // ROUNDS)
+            if step + PREFETCH < ALL_ROUNDS:
+                load_round(step + PREFETCH)

@@ -32,12 +32,14 @@ GROUPS = PACK * CH // P
 GROUP_CH = CH // GROUPS
 SUM_COLS = 24
 
+SCALAR_HALF = 1
 SUM_LAG = 1
 XI_LAG = ROUNDS + 1
 MX_LAG = 1
+FIRST_PIECES = 4
 PREFETCH = 3
 SHORT_ROUNDS = ALL_ROUNDS - XI_LAG
-WARM_PASSES = 28
+WARM_PASSES = 16
 FILL_PASSES = 4
 
 X_BUFS = XI_LAG - 1 + PREFETCH
@@ -59,6 +61,7 @@ def tile_covpool_pa_k_kernel(tc, x, out):
         xf_kept_pair_pool = ctx.enter_context(tc.tile_pool(name="xf_kept_pair", bufs=XF_KEPT))
         xf_kept_single_pool = ctx.enter_context(tc.tile_pool(name="xf_kept_single", bufs=2 * XF_KEPT))
         xi_quantised_pool = ctx.enter_context(tc.tile_pool(name="xi_quantised", bufs=2 * RUN // PAIR))
+        scalar_sums_pool = ctx.enter_context(tc.tile_pool(name="scalar_sums", bufs=2))
         mean_pool = ctx.enter_context(tc.tile_pool(name="mean", bufs=2))
         y_pool = ctx.enter_context(tc.tile_pool(name="y", bufs=2))
         ring = ctx.enter_context(tc.psum_pool(name="ring", bufs=5))
@@ -114,18 +117,23 @@ def tile_covpool_pa_k_kernel(tc, x, out):
         xf_kept = {}
         xi_quantised = {}
         sums_banks = {}
+        scalar_sums = {}
+        scalar_totals = {}
         spreads = {}
         mean_banks = {}
         neg_means = {}
         y_banks = {}
 
-        def load_round(rnd):
+        def load_round(rnd, pieces=1):
             b, r = divmod(rnd, ROUNDS)
             x_tile = x_pool.tile([P, HALVES, ROUND_K], BF16)
-            nc.sync.dma_start(
-                out=x_tile[:],
-                in_=positions[b, :, r * ROUND_K : (r + 1) * ROUND_K].rearrange("(h p) k -> p h k", p=P),
-            )
+            width = ROUND_K // pieces
+            for i in range(pieces):
+                first = r * ROUND_K + i * width
+                nc.sync.dma_start(
+                    out=x_tile[:, :, i * width : (i + 1) * width],
+                    in_=positions[b, :, first : first + width].rearrange("(h p) k -> p h k", p=P),
+                )
             x_tiles[rnd] = x_tile
 
         def transpose_pass(source, i, grouped, empty_bank):
@@ -153,14 +161,28 @@ def tile_covpool_pa_k_kernel(tc, x, out):
             if g == 0:
                 sums_bank = sums_psum.tile([P, SUM_COLS], F32)
                 sums_banks[b] = sums_bank
-            for q in range(GROUPS):
+            by_tensor = GROUPS // HALVES if g % RUN == RUN - 1 else GROUPS
+            for q in range(by_tensor):
                 nc.tensor.matmul(
                     sums_banks[b][:],
                     lhsT=xf_grouped[m][:, P * q : P * (q + 1)],
                     rhs=pick[:, q, :],
                     start=(g == 0 and q == 0),
-                    stop=(g == PASSES - 1 and q == GROUPS - 1),
+                    stop=(g == PASSES - 1 and q == by_tensor - 1),
                 )
+
+        def scalar_sum(rnd):
+            b, r = divmod(rnd, ROUNDS)
+            if r == 0:
+                columns = scalar_sums_pool.tile([P, ROUNDS], F32)
+                scalar_sums[b] = columns
+            copied = scalar_sums_pool.tile([P, K_PASS], BF16)
+            nc.scalar.activation(
+                out=copied[:],
+                in_=x_tiles[rnd][:, SCALAR_HALF, ROUND_K - K_PASS :],
+                func=mybir.ActivationFunctionType.Copy,
+                accum_out=scalar_sums[b][:, r : r + 1],
+            )
 
         def spread_sums(b):
             spread = mean_pool.tile([P, CH], F32)
@@ -171,6 +193,11 @@ def tile_covpool_pa_k_kernel(tc, x, out):
                 op=MULT,
             )
             spreads[b] = spread
+            total = mean_pool.tile([P, 1], F32)
+            nc.vector.tensor_reduce(out=total[:], in_=scalar_sums[b][:], axis=mybir.AxisListType.X, op=ADD)
+            diagonal = mean_pool.tile([P, P], F32)
+            nc.vector.tensor_scalar_mul(out=diagonal[:], in0=ident[:], scalar1=total[:])
+            scalar_totals[b] = diagonal
 
         def gather_means(b):
             mean_bank = ring.tile([P, HALVES], F32, tag="bank")
@@ -180,11 +207,26 @@ def tile_covpool_pa_k_kernel(tc, x, out):
                     lhsT=spreads[b][:, P * h : P * (h + 1)],
                     rhs=minus_inv_pos[:],
                     start=True,
-                    stop=True,
+                    stop=(h != SCALAR_HALF),
                 )
+                if h == SCALAR_HALF:
+                    nc.tensor.matmul(
+                        mean_bank[:, h : h + 1],
+                        lhsT=scalar_totals[b][:],
+                        rhs=minus_inv_pos[:],
+                        start=False,
+                        stop=True,
+                    )
             mean_banks[b] = mean_bank
             row_bank = ring.tile([P, CH], F32, tag="bank")
-            nc.tensor.matmul(row_bank[:], lhsT=spread_scale[:], rhs=spreads[b][:], start=True, stop=True)
+            nc.tensor.matmul(row_bank[:], lhsT=spread_scale[:], rhs=spreads[b][:], start=True, stop=False)
+            nc.tensor.matmul(
+                row_bank[:, P * SCALAR_HALF : P * (SCALAR_HALF + 1)],
+                lhsT=spread_scale[:],
+                rhs=scalar_totals[b][:],
+                start=False,
+                stop=True,
+            )
             mean_row = mean_pool.tile([P, CH], F32)
             nc.scalar.copy(out=mean_row[:], in_=row_bank[:])
             mean_rows[b] = mean_row
@@ -241,7 +283,7 @@ def tile_covpool_pa_k_kernel(tc, x, out):
             nc.sync.dma_start(out=out[b].rearrange("(h p) n -> p h n", p=P), in_=y_sb[:])
 
         for rnd in range(PREFETCH):
-            load_round(rnd)
+            load_round(rnd, FIRST_PIECES if rnd == 0 else 1)
 
         for step in range(ALL_ROUNDS + XI_LAG + MX_LAG):
             first_trip = step
@@ -271,18 +313,20 @@ def tile_covpool_pa_k_kernel(tc, x, out):
                     transpose_pass(
                         x_tiles[first_trip], i, xf_grouped[m], nc.vector.tensor_copy if by_vector else nc.scalar.copy
                     )
+            if first_trip < ALL_ROUNDS:
+                scalar_sum(first_trip)
             if 0 <= summed < ALL_ROUNDS:
                 for i in range(RUN):
                     add_to_sums(RUN * summed + i)
             elif first_trip < ALL_ROUNDS:
                 idle_passes(FILL_PASSES)
+            if summed_image >= 0:
+                spread_sums(summed_image)
             if first_trip < ALL_ROUNDS:
                 m = RUN * first_trip
                 xf_kept[m], xf_kept[m + 1] = quantise(xf_tiles[m], xf_kept_pair_pool, PAIR)
                 for i in range(PAIR, RUN):
                     xf_kept[m + i] = quantise(xf_tiles[m + i], xf_kept_single_pool, 1)[0]
-            if summed_image >= 0:
-                spread_sums(summed_image)
 
             if 0 <= second_trip < ALL_ROUNDS:
                 for i in range(RUN - 1 if short else RUN):

@@ -30,7 +30,7 @@ ALL_ROUNDS = IMAGES * ROUNDS
 ALL_PASSES = IMAGES * PASSES
 GROUPS = PACK * CH // P
 GROUP_CH = CH // GROUPS
-SUM_COLS = 24
+SUM_COLS = 28
 
 SCALAR_HALF = 1
 SUM_LAG = 1
@@ -39,7 +39,9 @@ MX_LAG = 1
 FIRST_PIECES = 4
 PREFETCH = 3
 SHORT_ROUNDS = ALL_ROUNDS - XI_LAG
-WARM_PASSES = 16
+WARM_PASSES = 20
+FIRST_FILL_PASSES = 8
+WAIT_PASSES = 5
 FILL_PASSES = 4
 
 X_BUFS = XI_LAG - 1 + PREFETCH
@@ -105,8 +107,6 @@ def tile_covpool_pa_k_kernel(tc, x, out):
         )
         minus_inv_pos = consts.tile([P, 1], F32)
         nc.vector.memset(minus_inv_pos[:], -1.0 / POS)
-        spread_scale = consts.tile([P, P], F32)
-        nc.vector.memset(spread_scale[:], -1.0 / (POS * POS))
 
         x_tiles = {}
         xi_tiles = {}
@@ -195,9 +195,7 @@ def tile_covpool_pa_k_kernel(tc, x, out):
             spreads[b] = spread
             total = mean_pool.tile([P, 1], F32)
             nc.vector.tensor_reduce(out=total[:], in_=scalar_sums[b][:], axis=mybir.AxisListType.X, op=ADD)
-            diagonal = mean_pool.tile([P, P], F32)
-            nc.vector.tensor_scalar_mul(out=diagonal[:], in0=ident[:], scalar1=total[:])
-            scalar_totals[b] = diagonal
+            scalar_totals[b] = total
 
         def gather_means(b):
             mean_bank = ring.tile([P, HALVES], F32, tag="bank")
@@ -207,28 +205,34 @@ def tile_covpool_pa_k_kernel(tc, x, out):
                     lhsT=spreads[b][:, P * h : P * (h + 1)],
                     rhs=minus_inv_pos[:],
                     start=True,
-                    stop=(h != SCALAR_HALF),
+                    stop=True,
                 )
-                if h == SCALAR_HALF:
-                    nc.tensor.matmul(
-                        mean_bank[:, h : h + 1],
-                        lhsT=scalar_totals[b][:],
-                        rhs=minus_inv_pos[:],
-                        start=False,
-                        stop=True,
-                    )
             mean_banks[b] = mean_bank
-            row_bank = ring.tile([P, CH], F32, tag="bank")
-            nc.tensor.matmul(row_bank[:], lhsT=spread_scale[:], rhs=spreads[b][:], start=True, stop=False)
-            nc.tensor.matmul(
-                row_bank[:, P * SCALAR_HALF : P * (SCALAR_HALF + 1)],
-                lhsT=spread_scale[:],
-                rhs=scalar_totals[b][:],
-                start=False,
-                stop=True,
+
+        def finish_means(b):
+            neg_mean = mean_pool.tile([P, HALVES], F32)
+            other = 1 - SCALAR_HALF
+            nc.vector.tensor_copy(out=neg_mean[:, other : other + 1], in_=mean_banks[b][:, other : other + 1])
+            nc.vector.scalar_tensor_tensor(
+                out=neg_mean[:, SCALAR_HALF : SCALAR_HALF + 1],
+                in0=scalar_totals[b][:],
+                scalar=-1.0 / POS,
+                in1=mean_banks[b][:, SCALAR_HALF : SCALAR_HALF + 1],
+                op0=MULT,
+                op1=ADD,
             )
+            neg_means[b] = neg_mean
+
+        def lay_means_along_rows(b):
+            row_bank = ring.tile([P, CH], F32, tag="bank")
+            for h in range(HALVES):
+                nc.tensor.transpose(
+                    row_bank[:, P * h : P * (h + 1)], neg_means[b][:, h : h + 1].to_broadcast([P, P]), ident[:]
+                )
             mean_row = mean_pool.tile([P, CH], F32)
-            nc.scalar.copy(out=mean_row[:], in_=row_bank[:])
+            nc.scalar.activation(
+                out=mean_row[:], in_=row_bank[:], func=mybir.ActivationFunctionType.Copy, scale=1.0 / POS
+            )
             mean_rows[b] = mean_row
 
         def form_xi(rnd):
@@ -292,8 +296,10 @@ def tile_covpool_pa_k_kernel(tc, x, out):
             multiplied = second_trip - MX_LAG
             summed_image = summed // ROUNDS if summed % ROUNDS == ROUNDS - 1 and summed < ALL_ROUNDS else -1
 
+            new_image = (summed - 1) // ROUNDS if summed > 0 and summed % ROUNDS == 0 and summed < ALL_ROUNDS else -1
+
             short = 0 <= second_trip < SHORT_ROUNDS
-            if short:
+            if short and new_image < 0:
                 form_transposed_xi(second_trip)
 
             if first_trip < ALL_ROUNDS:
@@ -313,13 +319,13 @@ def tile_covpool_pa_k_kernel(tc, x, out):
                     transpose_pass(
                         x_tiles[first_trip], i, xf_grouped[m], nc.vector.tensor_copy if by_vector else nc.scalar.copy
                     )
-            if first_trip < ALL_ROUNDS:
-                scalar_sum(first_trip)
+            if new_image >= 0:
+                lay_means_along_rows(new_image)
             if 0 <= summed < ALL_ROUNDS:
                 for i in range(RUN):
                     add_to_sums(RUN * summed + i)
             elif first_trip < ALL_ROUNDS:
-                idle_passes(FILL_PASSES)
+                idle_passes(FIRST_FILL_PASSES)
             if summed_image >= 0:
                 spread_sums(summed_image)
             if first_trip < ALL_ROUNDS:
@@ -327,6 +333,8 @@ def tile_covpool_pa_k_kernel(tc, x, out):
                 xf_kept[m], xf_kept[m + 1] = quantise(xf_tiles[m], xf_kept_pair_pool, PAIR)
                 for i in range(PAIR, RUN):
                     xf_kept[m + i] = quantise(xf_tiles[m + i], xf_kept_single_pool, 1)[0]
+            if short and new_image >= 0:
+                form_transposed_xi(second_trip)
 
             if 0 <= second_trip < ALL_ROUNDS:
                 for i in range(RUN - 1 if short else RUN):
@@ -336,6 +344,10 @@ def tile_covpool_pa_k_kernel(tc, x, out):
                         xi_pairs[m] = pair
                     grouped = xi_pairs[m - i % PAIR][:, PACK * CH * (i % PAIR) : PACK * CH * (i % PAIR + 1)]
                     transpose_pass(xi_tiles[second_trip], i, grouped, nc.scalar.copy)
+            if first_trip < ALL_ROUNDS:
+                scalar_sum(first_trip)
+            if summed_image == 0:
+                idle_passes(WAIT_PASSES)
             if summed_image >= 0:
                 gather_means(summed_image)
             if 0 <= multiplied < ALL_ROUNDS:
@@ -345,9 +357,7 @@ def tile_covpool_pa_k_kernel(tc, x, out):
                 idle_passes(FILL_PASSES)
 
             if summed_image >= 0:
-                neg_mean = mean_pool.tile([P, HALVES], F32)
-                nc.vector.tensor_copy(out=neg_mean[:], in_=mean_banks[summed_image][:])
-                neg_means[summed_image] = neg_mean
+                finish_means(summed_image)
             if 0 <= second_trip + 1 < ALL_ROUNDS:
                 form_xi(second_trip + 1)
             if 0 <= second_trip < ALL_ROUNDS:

@@ -35,14 +35,15 @@ SUM_COLS = 28
 SCALAR_HALF = 1
 SUM_LAG = 1
 XI_LAG = ROUNDS + 1
-MX_LAG = 1
+MX_LAG = 2
 FIRST_PIECES = 4
 PREFETCH = 3
 SHORT_ROUNDS = ALL_ROUNDS - XI_LAG
-WARM_PASSES = 20
-FIRST_FILL_PASSES = 8
-WAIT_PASSES = 5
-FILL_PASSES = 4
+WARM_PASSES = 28
+PIECE_FILL_PASSES = 6
+FIRST_FILL_PASSES = 12
+WAIT_PASSES = 10
+FILL_PASSES = 8
 
 X_BUFS = XI_LAG - 1 + PREFETCH
 XF_KEPT = XI_LAG + MX_LAG + 1
@@ -62,28 +63,28 @@ def tile_covpool_pa_k_kernel(tc, x, out):
         xi_pair_pool = ctx.enter_context(tc.tile_pool(name="xi_pair", bufs=3))
         xf_kept_pair_pool = ctx.enter_context(tc.tile_pool(name="xf_kept_pair", bufs=XF_KEPT))
         xf_kept_single_pool = ctx.enter_context(tc.tile_pool(name="xf_kept_single", bufs=2 * XF_KEPT))
-        xi_quantised_pool = ctx.enter_context(tc.tile_pool(name="xi_quantised", bufs=2 * RUN // PAIR))
+        xi_quantised_pool = ctx.enter_context(tc.tile_pool(name="xi_quantised", bufs=(MX_LAG + 1) * RUN // PAIR))
         scalar_sums_pool = ctx.enter_context(tc.tile_pool(name="scalar_sums", bufs=2))
         mean_pool = ctx.enter_context(tc.tile_pool(name="mean", bufs=2))
-        y_pool = ctx.enter_context(tc.tile_pool(name="y", bufs=2))
+        y_pool = ctx.enter_context(tc.tile_pool(name="y", bufs=1))
         ring = ctx.enter_context(tc.psum_pool(name="ring", bufs=5))
         sums_psum = ctx.enter_context(tc.psum_pool(name="sums", bufs=1))
         y_psum = ctx.enter_context(tc.psum_pool(name="products", bufs=1))
         ctx.enter_context(tc.manual_schedule())
 
-        zeros = consts.tile([P, PACK * CH], BF16, align_bytes=64)
-        zero_codes = consts.tile([P, CH], U32, align_bytes=64)
-        zero_scales = consts.tile([P, CH], U8, align_bytes=64)
+        zeros = consts.tile([P, PACK * P], BF16, align_bytes=64)
+        zero_codes = consts.tile([P, P], U32, align_bytes=64)
+        zero_scales = consts.tile([P, P], U8, align_bytes=64)
         nc.vector.memset(zeros[:].bitcast(I32), 0)
         nc.vector.quantize_mx(out=zero_codes[:].bitcast(FP8X4), scales=zero_scales[:], in_=zeros[:])
 
         def idle_passes(count):
-            idle_bank = ring.tile([P, CH], F32, tag="bank")
+            idle_bank = y_psum.tile([P, CH], F32, tag="y0")
             for w in range(count):
                 nc.tensor.matmul_mx(
-                    out=idle_bank[:],
-                    lhsT=zero_codes[:, 0:P].bitcast(FP8X4),
-                    lhsT_scale=zero_scales[:, 0:P],
+                    out=idle_bank[:, 0:P],
+                    lhsT=zero_codes[:].bitcast(FP8X4),
+                    lhsT_scale=zero_scales[:],
                     rhs=zero_codes[:].bitcast(FP8X4),
                     rhs_scale=zero_scales[:],
                     start=True,
@@ -153,7 +154,7 @@ def tile_covpool_pa_k_kernel(tc, x, out):
         def quantise(grouped, pool, count):
             codes = pool.tile([P, count * CH], U32, align_bytes=64)
             scales = pool.tile([P, count * CH], U8, align_bytes=64)
-            nc.vector.quantize_mx(out=codes[:].bitcast(FP8X4), scales=scales[:], in_=grouped[:])
+            nc.vector.quantize_mx(out=codes[:].bitcast(FP8X4), scales=scales[:], in_=grouped)
             return [(codes[:, CH * j : CH * (j + 1)], scales[:, CH * j : CH * (j + 1)]) for j in range(count)]
 
         def add_to_sums(m):
@@ -283,17 +284,24 @@ def tile_covpool_pa_k_kernel(tc, x, out):
         def store_image(b):
             y_sb = y_pool.tile([P, HALVES, CH], F32)
             for h in range(HALVES):
-                nc.vector.tensor_copy(out=y_sb[:, h, :], in_=y_banks[b, h][:])
-            nc.sync.dma_start(out=out[b].rearrange("(h p) n -> p h n", p=P), in_=y_sb[:])
+                empty_bank = nc.scalar.copy if b == IMAGES - 1 and h == 1 else nc.vector.tensor_copy
+                empty_bank(out=y_sb[:, h, :], in_=y_banks[b, h][:])
+                nc.sync.dma_start(out=out[b, P * h : P * (h + 1), :], in_=y_sb[:, h, :])
 
         for rnd in range(PREFETCH):
             load_round(rnd, FIRST_PIECES if rnd == 0 else 1)
 
-        for step in range(ALL_ROUNDS + XI_LAG + MX_LAG):
+        for step in range(ALL_ROUNDS + XI_LAG + 1):
             first_trip = step
             summed = first_trip - SUM_LAG
             second_trip = step - XI_LAG
-            multiplied = second_trip - MX_LAG
+            if step < ALL_ROUNDS:
+                products = [second_trip - MX_LAG]
+            elif step == ALL_ROUNDS:
+                products = [second_trip - MX_LAG, second_trip - 1]
+            else:
+                products = [second_trip - 1]
+            products = [r for r in products if 0 <= r < ALL_ROUNDS]
             summed_image = summed // ROUNDS if summed % ROUNDS == ROUNDS - 1 and summed < ALL_ROUNDS else -1
 
             new_image = (summed - 1) // ROUNDS if summed > 0 and summed % ROUNDS == 0 and summed < ALL_ROUNDS else -1
@@ -319,6 +327,8 @@ def tile_covpool_pa_k_kernel(tc, x, out):
                     transpose_pass(
                         x_tiles[first_trip], i, xf_grouped[m], nc.vector.tensor_copy if by_vector else nc.scalar.copy
                     )
+                    if first_trip == 0:
+                        idle_passes(PIECE_FILL_PASSES)
             if new_image >= 0:
                 lay_means_along_rows(new_image)
             if 0 <= summed < ALL_ROUNDS:
@@ -326,13 +336,17 @@ def tile_covpool_pa_k_kernel(tc, x, out):
                     add_to_sums(RUN * summed + i)
             elif first_trip < ALL_ROUNDS:
                 idle_passes(FIRST_FILL_PASSES)
+            passes = [RUN * r + i for r in products for i in range(RUN)]
+            early = RUN // 2 if step < ALL_ROUNDS and passes and passes[0] % PASSES > 0 else 0
+            for m in passes[:early]:
+                multiply_pass(m)
             if summed_image >= 0:
                 spread_sums(summed_image)
             if first_trip < ALL_ROUNDS:
                 m = RUN * first_trip
-                xf_kept[m], xf_kept[m + 1] = quantise(xf_tiles[m], xf_kept_pair_pool, PAIR)
+                xf_kept[m], xf_kept[m + 1] = quantise(xf_tiles[m][:], xf_kept_pair_pool, PAIR)
                 for i in range(PAIR, RUN):
-                    xf_kept[m + i] = quantise(xf_tiles[m + i], xf_kept_single_pool, 1)[0]
+                    xf_kept[m + i] = quantise(xf_tiles[m + i][:], xf_kept_single_pool, 1)[0]
             if short and new_image >= 0:
                 form_transposed_xi(second_trip)
 
@@ -343,17 +357,19 @@ def tile_covpool_pa_k_kernel(tc, x, out):
                         pair = xi_pair_pool.tile([P, PAIR * PACK * CH], BF16, align_bytes=64)
                         xi_pairs[m] = pair
                     grouped = xi_pairs[m - i % PAIR][:, PACK * CH * (i % PAIR) : PACK * CH * (i % PAIR + 1)]
-                    transpose_pass(xi_tiles[second_trip], i, grouped, nc.scalar.copy)
+                    by_vector = second_trip == ALL_ROUNDS - 1 and i == 1
+                    transpose_pass(
+                        xi_tiles[second_trip], i, grouped, nc.vector.tensor_copy if by_vector else nc.scalar.copy
+                    )
             if first_trip < ALL_ROUNDS:
                 scalar_sum(first_trip)
             if summed_image == 0:
                 idle_passes(WAIT_PASSES)
             if summed_image >= 0:
                 gather_means(summed_image)
-            if 0 <= multiplied < ALL_ROUNDS:
-                for i in range(RUN):
-                    multiply_pass(RUN * multiplied + i)
-            elif 0 <= second_trip < ALL_ROUNDS:
+            for m in passes[early:]:
+                multiply_pass(m)
+            if not passes and second_trip >= 0:
                 idle_passes(FILL_PASSES)
 
             if summed_image >= 0:
@@ -363,8 +379,14 @@ def tile_covpool_pa_k_kernel(tc, x, out):
             if 0 <= second_trip < ALL_ROUNDS:
                 for i in range(0, RUN, PAIR):
                     m = RUN * second_trip + i
-                    xi_quantised[m], xi_quantised[m + 1] = quantise(xi_pairs[m], xi_quantised_pool, PAIR)
-            if 0 <= multiplied < ALL_ROUNDS and multiplied % ROUNDS == ROUNDS - 1:
-                store_image(multiplied // ROUNDS)
+                    if m < ALL_PASSES - PAIR:
+                        xi_quantised[m], xi_quantised[m + 1] = quantise(xi_pairs[m][:], xi_quantised_pool, PAIR)
+                    else:
+                        for j in range(PAIR):
+                            half = xi_pairs[m][:, PACK * CH * j : PACK * CH * (j + 1)]
+                            xi_quantised[m + j] = quantise(half, xi_quantised_pool, 1)[0]
+            for r in products:
+                if r % ROUNDS == ROUNDS - 1:
+                    store_image(r // ROUNDS)
             if step + PREFETCH < ALL_ROUNDS:
                 load_round(step + PREFETCH)

@@ -35,13 +35,13 @@ SUM_COLS = 28
 SCALAR_HALF = 1
 SUM_LAG = 1
 XI_LAG = ROUNDS + 1
-MX_LAG = 2
+MX_LAG = 1
 FIRST_PIECES = 4
 PREFETCH = 3
 SHORT_ROUNDS = ALL_ROUNDS - XI_LAG
 WARM_PASSES = 28
-PIECE_FILL_PASSES = 6
-FIRST_FILL_PASSES = 12
+PIECE_FILL_PASSES = 4
+FIRST_FILL_PASSES = 10
 WAIT_PASSES = 10
 FILL_PASSES = 8
 
@@ -288,105 +288,108 @@ def tile_covpool_pa_k_kernel(tc, x, out):
                 empty_bank(out=y_sb[:, h, :], in_=y_banks[b, h][:])
                 nc.sync.dma_start(out=out[b, P * h : P * (h + 1), :], in_=y_sb[:, h, :])
 
+        def transpose_first_trip(rnd, vector_helps):
+            for i in range(RUN):
+                m = RUN * rnd + i
+                if i == 0:
+                    pair = xf_pair_pool.tile([P, PAIR * PACK * CH], BF16, align_bytes=64)
+                    xf_tiles[m] = pair
+                elif i == PAIR:
+                    single = xf_single_pool.tile([P, PACK * CH], BF16, align_bytes=64)
+                    xf_tiles[m] = single
+                elif i == RUN - 1:
+                    last = xf_last_pool.tile([P, PACK * CH], BF16, align_bytes=64)
+                    xf_tiles[m] = last
+                xf_grouped[m] = pair[:, PACK * CH * i : PACK * CH * (i + 1)] if i < PAIR else xf_tiles[m][:]
+                by_vector = vector_helps and i == RUN - 1
+                transpose_pass(x_tiles[rnd], i, xf_grouped[m], nc.vector.tensor_copy if by_vector else nc.scalar.copy)
+                if rnd == 0:
+                    idle_passes(PIECE_FILL_PASSES)
+
+        def quantise_first_trip(rnd):
+            m = RUN * rnd
+            xf_kept[m], xf_kept[m + 1] = quantise(xf_tiles[m][:], xf_kept_pair_pool, PAIR)
+            for i in range(PAIR, RUN):
+                xf_kept[m + i] = quantise(xf_tiles[m + i][:], xf_kept_single_pool, 1)[0]
+
+        def transpose_second_trip(rnd):
+            for i in range(RUN - 1 if rnd < SHORT_ROUNDS else RUN):
+                m = RUN * rnd + i
+                if m not in xi_pairs and i % PAIR == 0:
+                    pair = xi_pair_pool.tile([P, PAIR * PACK * CH], BF16, align_bytes=64)
+                    xi_pairs[m] = pair
+                grouped = xi_pairs[m - i % PAIR][:, PACK * CH * (i % PAIR) : PACK * CH * (i % PAIR + 1)]
+                by_vector = rnd == ALL_ROUNDS - 1 and i == 1
+                transpose_pass(xi_tiles[rnd], i, grouped, nc.vector.tensor_copy if by_vector else nc.scalar.copy)
+
+        def quantise_second_trip(rnd):
+            for i in range(0, RUN, PAIR):
+                m = RUN * rnd + i
+                if m < ALL_PASSES - PAIR:
+                    xi_quantised[m], xi_quantised[m + 1] = quantise(xi_pairs[m][:], xi_quantised_pool, PAIR)
+                else:
+                    for j in range(PAIR):
+                        half = xi_pairs[m][:, PACK * CH * j : PACK * CH * (j + 1)]
+                        xi_quantised[m + j] = quantise(half, xi_quantised_pool, 1)[0]
+
         for rnd in range(PREFETCH):
             load_round(rnd, FIRST_PIECES if rnd == 0 else 1)
 
-        for step in range(ALL_ROUNDS + XI_LAG + 1):
-            first_trip = step
-            summed = first_trip - SUM_LAG
-            second_trip = step - XI_LAG
-            if step < ALL_ROUNDS:
-                products = [second_trip - MX_LAG]
-            elif step == ALL_ROUNDS:
-                products = [second_trip - MX_LAG, second_trip - 1]
-            else:
-                products = [second_trip - 1]
-            products = [r for r in products if 0 <= r < ALL_ROUNDS]
-            summed_image = summed // ROUNDS if summed % ROUNDS == ROUNDS - 1 and summed < ALL_ROUNDS else -1
-
-            new_image = (summed - 1) // ROUNDS if summed > 0 and summed % ROUNDS == 0 and summed < ALL_ROUNDS else -1
-
+        for step in range(ALL_ROUNDS + XI_LAG + MX_LAG):
+            first_trip = step if step < ALL_ROUNDS else -1
+            summed = step - SUM_LAG if step - SUM_LAG < ALL_ROUNDS else -1
+            second_trip = step - XI_LAG if step - XI_LAG < ALL_ROUNDS else -1
+            multiplied = step - XI_LAG - MX_LAG
+            summed_image = summed // ROUNDS if summed >= 0 and summed % ROUNDS == ROUNDS - 1 else -1
+            new_image = summed // ROUNDS - 1 if summed > 0 and summed % ROUNDS == 0 else -1
             short = 0 <= second_trip < SHORT_ROUNDS
-            if short and new_image < 0:
-                form_transposed_xi(second_trip)
+            second_first = short and new_image < 0
 
-            if first_trip < ALL_ROUNDS:
-                for i in range(RUN):
-                    m = RUN * first_trip + i
-                    if i == 0:
-                        pair = xf_pair_pool.tile([P, PAIR * PACK * CH], BF16, align_bytes=64)
-                        xf_tiles[m] = pair
-                    elif i == PAIR:
-                        single = xf_single_pool.tile([P, PACK * CH], BF16, align_bytes=64)
-                        xf_tiles[m] = single
-                    elif i == RUN - 1:
-                        last = xf_last_pool.tile([P, PACK * CH], BF16, align_bytes=64)
-                        xf_tiles[m] = last
-                    xf_grouped[m] = pair[:, PACK * CH * i : PACK * CH * (i + 1)] if i < PAIR else xf_tiles[m][:]
-                    by_vector = i == RUN - 1 and not short
-                    transpose_pass(
-                        x_tiles[first_trip], i, xf_grouped[m], nc.vector.tensor_copy if by_vector else nc.scalar.copy
-                    )
-                    if first_trip == 0:
-                        idle_passes(PIECE_FILL_PASSES)
+            if 0 <= step - XI_LAG + 1 < ALL_ROUNDS and summed_image < 0:
+                form_xi(step - XI_LAG + 1)
+            if second_first:
+                form_transposed_xi(second_trip)
+                transpose_second_trip(second_trip)
+            elif first_trip >= 0:
+                transpose_first_trip(first_trip, not short)
             if new_image >= 0:
                 lay_means_along_rows(new_image)
-            if 0 <= summed < ALL_ROUNDS:
+            if summed >= 0:
                 for i in range(RUN):
                     add_to_sums(RUN * summed + i)
-            elif first_trip < ALL_ROUNDS:
+            elif first_trip >= 0:
                 idle_passes(FIRST_FILL_PASSES)
-            passes = [RUN * r + i for r in products for i in range(RUN)]
-            early = RUN // 2 if step < ALL_ROUNDS and passes and passes[0] % PASSES > 0 else 0
-            for m in passes[:early]:
-                multiply_pass(m)
             if summed_image >= 0:
                 spread_sums(summed_image)
-            if first_trip < ALL_ROUNDS:
-                m = RUN * first_trip
-                xf_kept[m], xf_kept[m + 1] = quantise(xf_tiles[m][:], xf_kept_pair_pool, PAIR)
-                for i in range(PAIR, RUN):
-                    xf_kept[m + i] = quantise(xf_tiles[m + i][:], xf_kept_single_pool, 1)[0]
-            if short and new_image >= 0:
-                form_transposed_xi(second_trip)
-
-            if 0 <= second_trip < ALL_ROUNDS:
-                for i in range(RUN - 1 if short else RUN):
-                    m = RUN * second_trip + i
-                    if i == 0 or i == PAIR and not short:
-                        pair = xi_pair_pool.tile([P, PAIR * PACK * CH], BF16, align_bytes=64)
-                        xi_pairs[m] = pair
-                    grouped = xi_pairs[m - i % PAIR][:, PACK * CH * (i % PAIR) : PACK * CH * (i % PAIR + 1)]
-                    by_vector = second_trip == ALL_ROUNDS - 1 and i == 1
-                    transpose_pass(
-                        xi_tiles[second_trip], i, grouped, nc.vector.tensor_copy if by_vector else nc.scalar.copy
-                    )
-            if first_trip < ALL_ROUNDS:
+            if second_first:
+                transpose_first_trip(first_trip, False)
+                quantise_second_trip(second_trip)
+            else:
+                if first_trip >= 0:
+                    quantise_first_trip(first_trip)
+                if short:
+                    form_transposed_xi(second_trip)
+                if second_trip >= 0:
+                    transpose_second_trip(second_trip)
+            if first_trip >= 0:
                 scalar_sum(first_trip)
             if summed_image == 0:
                 idle_passes(WAIT_PASSES)
             if summed_image >= 0:
                 gather_means(summed_image)
-            for m in passes[early:]:
-                multiply_pass(m)
-            if not passes and second_trip >= 0:
+            if multiplied >= 0:
+                for i in range(RUN):
+                    multiply_pass(RUN * multiplied + i)
+            elif second_trip >= 0:
                 idle_passes(FILL_PASSES)
-
             if summed_image >= 0:
                 finish_means(summed_image)
-            if 0 <= second_trip + 1 < ALL_ROUNDS:
-                form_xi(second_trip + 1)
-            if 0 <= second_trip < ALL_ROUNDS:
-                for i in range(0, RUN, PAIR):
-                    m = RUN * second_trip + i
-                    if m < ALL_PASSES - PAIR:
-                        xi_quantised[m], xi_quantised[m + 1] = quantise(xi_pairs[m][:], xi_quantised_pool, PAIR)
-                    else:
-                        for j in range(PAIR):
-                            half = xi_pairs[m][:, PACK * CH * j : PACK * CH * (j + 1)]
-                            xi_quantised[m + j] = quantise(half, xi_quantised_pool, 1)[0]
-            for r in products:
-                if r % ROUNDS == ROUNDS - 1:
-                    store_image(r // ROUNDS)
+                form_xi(step - XI_LAG + 1)
+            if second_first:
+                quantise_first_trip(first_trip)
+            elif second_trip >= 0:
+                quantise_second_trip(second_trip)
+            if multiplied >= 0 and multiplied % ROUNDS == ROUNDS - 1:
+                store_image(multiplied // ROUNDS)
             if step + PREFETCH < ALL_ROUNDS:
                 load_round(step + PREFETCH)

from contextlib import ExitStack

import concourse.mybir as mybir
from concourse.masks import make_identity

FLOPS = 2 * 4 * 256 * 256 * 16384

BF16 = mybir.dt.bfloat16
F32 = mybir.dt.float32
U32 = mybir.dt.uint32
U8 = mybir.dt.uint8
I32 = mybir.dt.int32
FP8X4 = mybir.dt.float8_e4m3fn_x4
ADD = mybir.AluOpType.add
MULT = mybir.AluOpType.mult

P = 128
PACK = 4
K_PASS = P * PACK
IMAGES = 4
CH = 256
HALVES = CH // P
POS = 128 * 128
PASSES = POS // K_PASS
PAIR = 2
RUN = 4
ROUND_K = RUN * K_PASS
ROUNDS = PASSES // RUN
ALL_ROUNDS = IMAGES * ROUNDS
ALL_PASSES = IMAGES * PASSES
GROUPS = PACK * CH // P
GROUP_CH = CH // GROUPS
SUM_COLS = 28

SCALAR_HALF = 1
SUM_LAG = 1
XI_LAG = ROUNDS + 1
MX_LAG = 1
FIRST_PIECES = 4
PREFETCH = 3
SHORT_ROUNDS = ALL_ROUNDS - XI_LAG
WARM_PASSES = 28
PIECE_FILL_PASSES = 4
FIRST_FILL_PASSES = 10
WAIT_PASSES = 10
FILL_PASSES = 8

X_BUFS = XI_LAG - 1 + PREFETCH
XF_KEPT = XI_LAG + MX_LAG + 1


def tile_covpool_pa_k_kernel(tc, x, out):
    nc = tc.nc
    positions = x.rearrange("b c i j -> b c (i j)")

    with ExitStack() as ctx:
        consts = ctx.enter_context(tc.tile_pool(name="consts", bufs=1))
        x_pool = ctx.enter_context(tc.tile_pool(name="x", bufs=X_BUFS))
        xi_pool = ctx.enter_context(tc.tile_pool(name="xi", bufs=2))
        xf_pair_pool = ctx.enter_context(tc.tile_pool(name="xf_pair", bufs=1 + SUM_LAG))
        xf_single_pool = ctx.enter_context(tc.tile_pool(name="xf_single", bufs=1 + SUM_LAG))
        xf_last_pool = ctx.enter_context(tc.tile_pool(name="xf_last", bufs=XI_LAG + 1))
        xi_pair_pool = ctx.enter_context(tc.tile_pool(name="xi_pair", bufs=3))
        xf_kept_pair_pool = ctx.enter_context(tc.tile_pool(name="xf_kept_pair", bufs=XF_KEPT))
        xf_kept_single_pool = ctx.enter_context(tc.tile_pool(name="xf_kept_single", bufs=2 * XF_KEPT))
        xi_quantised_pool = ctx.enter_context(tc.tile_pool(name="xi_quantised", bufs=(MX_LAG + 1) * RUN // PAIR))
        scalar_sums_pool = ctx.enter_context(tc.tile_pool(name="scalar_sums", bufs=2))
        mean_pool = ctx.enter_context(tc.tile_pool(name="mean", bufs=2))
        y_pool = ctx.enter_context(tc.tile_pool(name="y", bufs=1))
        ring = ctx.enter_context(tc.psum_pool(name="ring", bufs=5))
        sums_psum = ctx.enter_context(tc.psum_pool(name="sums", bufs=1))
        y_psum = ctx.enter_context(tc.psum_pool(name="products", bufs=1))
        ctx.enter_context(tc.manual_schedule())

        zeros = consts.tile([P, PACK * P], BF16, align_bytes=64)
        zero_codes = consts.tile([P, P], U32, align_bytes=64)
        zero_scales = consts.tile([P, P], U8, align_bytes=64)
        nc.vector.memset(zeros[:].bitcast(I32), 0)
        nc.vector.quantize_mx(out=zero_codes[:].bitcast(FP8X4), scales=zero_scales[:], in_=zeros[:])

        def idle_passes(count):
            idle_bank = y_psum.tile([P, CH], F32, tag="y0")
            for w in range(count):
                nc.tensor.matmul_mx(
                    out=idle_bank[:, 0:P],
                    lhsT=zero_codes[:].bitcast(FP8X4),
                    lhsT_scale=zero_scales[:],
                    rhs=zero_codes[:].bitcast(FP8X4),
                    rhs_scale=zero_scales[:],
                    start=True,
                    stop=True,
                )

        idle_passes(WARM_PASSES)

        ident = consts.tile([P, P], F32)
        make_identity(nc, ident[:])
        pick = consts.tile([P, GROUPS, SUM_COLS], BF16)
        nc.vector.memset(pick[:], 0.0)
        for q in range(GROUPS):
            nc.vector.memset(pick[:, q, q : q + 1], 1.0)
        same_channel = consts.tile([P, GROUP_CH], F32)
        nc.vector.tensor_reduce(
            out=same_channel[:],
            in_=ident[:].rearrange("p (c t) -> p c t", t=PACK),
            axis=mybir.AxisListType.X,
            op=ADD,
        )
        minus_inv_pos = consts.tile([P, 1], F32)
        nc.vector.memset(minus_inv_pos[:], -1.0 / POS)

        x_tiles = {}
        xi_tiles = {}
        xf_grouped = {}
        xf_tiles = {}
        xi_pairs = {}
        mean_rows = {}
        xf_kept = {}
        xi_quantised = {}
        sums_banks = {}
        scalar_sums = {}
        scalar_totals = {}
        spreads = {}
        mean_banks = {}
        neg_means = {}
        y_banks = {}

        def load_round(rnd, pieces=1):
            b, r = divmod(rnd, ROUNDS)
            x_tile = x_pool.tile([P, HALVES, ROUND_K], BF16)
            width = ROUND_K // pieces
            for i in range(pieces):
                first = r * ROUND_K + i * width
                nc.sync.dma_start(
                    out=x_tile[:, :, i * width : (i + 1) * width],
                    in_=positions[b, :, first : first + width].rearrange("(h p) k -> p h k", p=P),
                )
            x_tiles[rnd] = x_tile

        def transpose_pass(source, i, grouped, empty_bank):
            words = source[:].bitcast(F32)
            bank = ring.tile([P, 2, CH], F32, tag="bank")
            for h in range(HALVES):
                for u in range(2):
                    first = (K_PASS // 2) * i + P * u
                    nc.tensor.transpose(
                        bank[:, u, P * h : P * (h + 1)], words[:, h, first : first + P], ident[:]
                    )
            empty_bank(
                out=grouped.bitcast(F32).rearrange("p (c u) -> p c u", u=2),
                in_=bank[:].rearrange("p u c -> p c u"),
            )

        def quantise(grouped, pool, count):
            codes = pool.tile([P, count * CH], U32, align_bytes=64)
            scales = pool.tile([P, count * CH], U8, align_bytes=64)
            nc.vector.quantize_mx(out=codes[:].bitcast(FP8X4), scales=scales[:], in_=grouped)
            return [(codes[:, CH * j : CH * (j + 1)], scales[:, CH * j : CH * (j + 1)]) for j in range(count)]

        def add_to_sums(m):
            b, g = divmod(m, PASSES)
            if g == 0:
                sums_bank = sums_psum.tile([P, SUM_COLS], F32)
                sums_banks[b] = sums_bank
            by_tensor = GROUPS // HALVES if g % RUN == RUN - 1 else GROUPS
            for q in range(by_tensor):
                nc.tensor.matmul(
                    sums_banks[b][:],
                    lhsT=xf_grouped[m][:, P * q : P * (q + 1)],
                    rhs=pick[:, q, :],
                    start=(g == 0 and q == 0),
                    stop=(g == PASSES - 1 and q == by_tensor - 1),
                )

        def scalar_sum(rnd):
            b, r = divmod(rnd, ROUNDS)
            if r == 0:
                columns = scalar_sums_pool.tile([P, ROUNDS], F32)
                scalar_sums[b] = columns
            copied = scalar_sums_pool.tile([P, K_PASS], BF16)
            nc.scalar.activation(
                out=copied[:],
                in_=x_tiles[rnd][:, SCALAR_HALF, ROUND_K - K_PASS :],
                func=mybir.ActivationFunctionType.Copy,
                accum_out=scalar_sums[b][:, r : r + 1],
            )

        def spread_sums(b):
            spread = mean_pool.tile([P, CH], F32)
            nc.vector.tensor_tensor(
                out=spread[:].rearrange("p (q c) -> p q c", q=GROUPS),
                in0=same_channel[:].unsqueeze(1).to_broadcast([P, GROUPS, GROUP_CH]),
                in1=sums_banks[b][:, 0:GROUPS].unsqueeze(2).to_broadcast([P, GROUPS, GROUP_CH]),
                op=MULT,
            )
            spreads[b] = spread
            total = mean_pool.tile([P, 1], F32)
            nc.vector.tensor_reduce(out=total[:], in_=scalar_sums[b][:], axis=mybir.AxisListType.X, op=ADD)
            scalar_totals[b] = total

        def gather_means(b):
            mean_bank = ring.tile([P, HALVES], F32, tag="bank")
            for h in range(HALVES):
                nc.tensor.matmul(
                    mean_bank[:, h : h + 1],
                    lhsT=spreads[b][:, P * h : P * (h + 1)],
                    rhs=minus_inv_pos[:],
                    start=True,
                    stop=True,
                )
            mean_banks[b] = mean_bank

        def finish_means(b):
            neg_mean = mean_pool.tile([P, HALVES], F32)
            other = 1 - SCALAR_HALF
            nc.vector.tensor_copy(out=neg_mean[:, other : other + 1], in_=mean_banks[b][:, other : other + 1])
            nc.vector.scalar_tensor_tensor(
                out=neg_mean[:, SCALAR_HALF : SCALAR_HALF + 1],
                in0=scalar_totals[b][:],
                scalar=-1.0 / POS,
                in1=mean_banks[b][:, SCALAR_HALF : SCALAR_HALF + 1],
                op0=MULT,
                op1=ADD,
            )
            neg_means[b] = neg_mean

        def lay_means_along_rows(b):
            row_bank = ring.tile([P, CH], F32, tag="bank")
            for h in range(HALVES):
                nc.tensor.transpose(
                    row_bank[:, P * h : P * (h + 1)], neg_means[b][:, h : h + 1].to_broadcast([P, P]), ident[:]
                )
            mean_row = mean_pool.tile([P, CH], F32)
            nc.scalar.activation(
                out=mean_row[:], in_=row_bank[:], func=mybir.ActivationFunctionType.Copy, scale=1.0 / POS
            )
            mean_rows[b] = mean_row

        def form_xi(rnd):
            b = rnd // ROUNDS
            xi_tile = xi_pool.tile([P, HALVES, ROUND_K], BF16)
            width = (RUN - 1 if rnd < SHORT_ROUNDS else RUN) * K_PASS
            for h in range(HALVES):
                nc.vector.tensor_scalar(
                    out=xi_tile[:, h, 0:width],
                    in0=x_tiles[rnd][:, h, 0:width],
                    scalar1=neg_means[b][:, h : h + 1],
                    scalar2=1.0 / POS,
                    op0=ADD,
                    op1=MULT,
                )
            xi_tiles[rnd] = xi_tile

        def form_transposed_xi(rnd):
            pair = xi_pair_pool.tile([P, PAIR * PACK * CH], BF16, align_bytes=64)
            nc.vector.scalar_tensor_tensor(
                out=pair[:, PACK * CH :].rearrange("p (c t) -> p c t", t=PACK),
                in0=xf_tiles[RUN * rnd + RUN - 1][:].rearrange("p (c t) -> p c t", t=PACK),
                scalar=1.0 / POS,
                in1=mean_rows[rnd // ROUNDS][:].unsqueeze(2).to_broadcast([P, CH, PACK]),
                op0=MULT,
                op1=ADD,
            )
            xi_pairs[RUN * rnd + RUN - PAIR] = pair

        def multiply_pass(m):
            b, g = divmod(m, PASSES)
            xi_codes, xi_scales = xi_quantised[m]
            xf_codes, xf_scales = xf_kept[m]
            for h in range(HALVES):
                if g == 0:
                    y_bank = y_psum.tile([P, CH], F32, tag="y%d" % h)
                    y_banks[b, h] = y_bank
                nc.tensor.matmul_mx(
                    out=y_banks[b, h][:],
                    lhsT=xi_codes[:, P * h : P * (h + 1)].bitcast(FP8X4),
                    lhsT_scale=xi_scales[:, P * h : P * (h + 1)],
                    rhs=xf_codes.bitcast(FP8X4),
                    rhs_scale=xf_scales,
                    start=(g == 0),
                    stop=(g == PASSES - 1),
                )

        def store_image(b):
            y_sb = y_pool.tile([P, HALVES, CH], F32)
            for h in range(HALVES):
                empty_bank = nc.scalar.copy if b == IMAGES - 1 and h == 1 else nc.vector.tensor_copy
                empty_bank(out=y_sb[:, h, :], in_=y_banks[b, h][:])
                nc.sync.dma_start(out=out[b, P * h : P * (h + 1), :], in_=y_sb[:, h, :])

        def transpose_first_trip(rnd, vector_helps):
            for i in range(RUN):
                m = RUN * rnd + i
                if i == 0:
                    pair = xf_pair_pool.tile([P, PAIR * PACK * CH], BF16, align_bytes=64)
                    xf_tiles[m] = pair
                elif i == PAIR:
                    single = xf_single_pool.tile([P, PACK * CH], BF16, align_bytes=64)
                    xf_tiles[m] = single
                elif i == RUN - 1:
                    last = xf_last_pool.tile([P, PACK * CH], BF16, align_bytes=64)
                    xf_tiles[m] = last
                xf_grouped[m] = pair[:, PACK * CH * i : PACK * CH * (i + 1)] if i < PAIR else xf_tiles[m][:]
                by_vector = vector_helps and i == RUN - 1
                transpose_pass(x_tiles[rnd], i, xf_grouped[m], nc.vector.tensor_copy if by_vector else nc.scalar.copy)
                if rnd == 0:
                    idle_passes(PIECE_FILL_PASSES)

        def quantise_first_trip(rnd):
            m = RUN * rnd
            xf_kept[m], xf_kept[m + 1] = quantise(xf_tiles[m][:], xf_kept_pair_pool, PAIR)
            for i in range(PAIR, RUN):
                xf_kept[m + i] = quantise(xf_tiles[m + i][:], xf_kept_single_pool, 1)[0]

        def transpose_second_trip(rnd):
            for i in range(RUN - 1 if rnd < SHORT_ROUNDS else RUN):
                m = RUN * rnd + i
                if m not in xi_pairs and i % PAIR == 0:
                    pair = xi_pair_pool.tile([P, PAIR * PACK * CH], BF16, align_bytes=64)
                    xi_pairs[m] = pair
                grouped = xi_pairs[m - i % PAIR][:, PACK * CH * (i % PAIR) : PACK * CH * (i % PAIR + 1)]
                by_vector = rnd == ALL_ROUNDS - 1 and i == 1
                transpose_pass(xi_tiles[rnd], i, grouped, nc.vector.tensor_copy if by_vector else nc.scalar.copy)

        def quantise_second_trip(rnd):
            for i in range(0, RUN, PAIR):
                m = RUN * rnd + i
                if m < ALL_PASSES - PAIR:
                    xi_quantised[m], xi_quantised[m + 1] = quantise(xi_pairs[m][:], xi_quantised_pool, PAIR)
                else:
                    for j in range(PAIR):
                        half = xi_pairs[m][:, PACK * CH * j : PACK * CH * (j + 1)]
                        xi_quantised[m + j] = quantise(half, xi_quantised_pool, 1)[0]

        for rnd in range(PREFETCH):
            load_round(rnd, FIRST_PIECES if rnd == 0 else 1)

        for step in range(ALL_ROUNDS + XI_LAG + MX_LAG):
            first_trip = step if step < ALL_ROUNDS else -1
            summed = step - SUM_LAG if step - SUM_LAG < ALL_ROUNDS else -1
            second_trip = step - XI_LAG if step - XI_LAG < ALL_ROUNDS else -1
            multiplied = step - XI_LAG - MX_LAG
            summed_image = summed // ROUNDS if summed >= 0 and summed % ROUNDS == ROUNDS - 1 else -1
            new_image = summed // ROUNDS - 1 if summed > 0 and summed % ROUNDS == 0 else -1
            short = 0 <= second_trip < SHORT_ROUNDS
            second_first = short and new_image < 0

            if 0 <= step - XI_LAG + 1 < ALL_ROUNDS and summed_image < 0:
                form_xi(step - XI_LAG + 1)
            if second_first:
                form_transposed_xi(second_trip)
                transpose_second_trip(second_trip)
            elif first_trip >= 0:
                transpose_first_trip(first_trip, not short)
            if new_image >= 0:
                lay_means_along_rows(new_image)
            if summed >= 0:
                for i in range(RUN):
                    add_to_sums(RUN * summed + i)
            elif first_trip >= 0:
                idle_passes(FIRST_FILL_PASSES)
            if summed_image >= 0:
                spread_sums(summed_image)
            if second_first:
                transpose_first_trip(first_trip, False)
                quantise_second_trip(second_trip)
            else:
                if first_trip >= 0:
                    quantise_first_trip(first_trip)
                if short:
                    form_transposed_xi(second_trip)
                if second_trip >= 0:
                    transpose_second_trip(second_trip)
            if first_trip >= 0:
                scalar_sum(first_trip)
            if summed_image == 0:
                idle_passes(WAIT_PASSES)
            if summed_image >= 0:
                gather_means(summed_image)
            if multiplied >= 0:
                for i in range(RUN):
                    multiply_pass(RUN * multiplied + i)
            elif second_trip >= 0:
                idle_passes(FILL_PASSES)
            if summed_image >= 0:
                finish_means(summed_image)
                form_xi(step - XI_LAG + 1)
            if second_first:
                quantise_first_trip(first_trip)
            elif second_trip >= 0:
                quantise_second_trip(second_trip)
            if multiplied >= 0 and multiplied % ROUNDS == ROUNDS - 1:
                store_image(multiplied // ROUNDS)
            if step + PREFETCH < ALL_ROUNDS:
                load_round(step + PREFETCH)
